import numpy as np
import ml_dtypes


def mxq(x, axis, fmt="e4m3"):
    dtype, down = {"e4m3": (ml_dtypes.float8_e4m3fn, 7), "e5m2": (ml_dtypes.float8_e5m2, 14)}[fmt]
    v = np.moveaxis(np.asarray(x, np.float32).astype(ml_dtypes.bfloat16).astype(np.float64), axis, -1)
    blocks = v.reshape(v.shape[:-1] + (-1, 32))
    amax = np.abs(blocks).max(-1, keepdims=True)
    byte = np.maximum(np.where(amax > 0, np.frexp(amax)[1] - 1 + 127, 0) - down, 1)
    scale = np.exp2(byte - 127.0)
    codes = (blocks / scale).astype(np.float32).astype(dtype).astype(np.float64)
    return np.moveaxis((codes * scale).reshape(v.shape), -1, axis)


WIDE = False


def mx_kscale(k):
    if not WIDE:
        return np.ones(k)
    levels = np.array([10, -10, 5, -5, 0])
    a = np.random.permutation(np.resize(levels, k // 512 * 4)).reshape(k // 512, 4)
    idx = np.arange(k)
    return np.exp2(a[idx // 512, idx % 128 // 32])


BF16 = ml_dtypes.bfloat16


def bf(x):
    return np.asarray(x, np.float32).astype(BF16)


def f64(x):
    return np.asarray(x).astype(np.float64)


B, S, D, E, HD = 2, 512, 512, 512, 64
ROPE_BASE = 10000.0


def rope_tables():
    inv_freq = 1.0 / ROPE_BASE ** (np.arange(0, E, 2) / E)
    ang = np.repeat(np.arange(S)[:, None] * inv_freq[None, :], 2, axis=-1)
    return np.cos(ang), np.sin(ang)


def rotate_half(v):
    h = v.shape[-1] // 2
    return np.concatenate([-v[..., h:], v[..., :h]], axis=-1)


def setup_inputs():
    s = mx_kscale(D)
    return {"x": bf(np.random.standard_normal((B, S, D)) * s),
            "Wq": bf(np.random.standard_normal((D, E)) * 0.5 / np.sqrt(D) / s[:, None]),
            "bq": bf(np.random.standard_normal(E) * 0.1),
            "Wk": bf(np.random.standard_normal((D, E)) * 0.5 / np.sqrt(D) / s[:, None]),
            "bk": bf(np.random.standard_normal(E) * 0.1)}


def reference(x, Wq, bq, Wk, bk):
    xq = mxq(f64(x), 2, "e4m3")
    q = (xq @ mxq(f64(Wq), 0, "e4m3")) + f64(bq)
    k = (xq @ mxq(f64(Wk), 0, "e4m3")) + f64(bk)
    cos, sin = rope_tables()
    qr = q * cos + rotate_half(q) * sin
    kr = k * cos + rotate_half(k) * sin
    return qr, kr

@@ -1,0 +1,282 @@
+import math
+from contextlib import ExitStack
+
+import concourse.mybir as mybir
+from concourse.masks import make_identity
+
+F32 = mybir.dt.float32
+BF16 = mybir.dt.bfloat16
+U32 = mybir.dt.uint32
+U8 = mybir.dt.uint8
+FP8X4 = mybir.dt.float8_e4m3fn_x4
+ALU = mybir.AluOpType
+ACT = mybir.ActivationFunctionType
+
+P = 128
+PACK = 4
+BATCH = 2
+SEQ = 512
+DIM = 512
+FEAT = 512
+PROJECTIONS = 2
+TOKEN_TILES = SEQ // P
+TOKEN_PAIRS = TOKEN_TILES // 2
+HALVES = 2
+HALF = FEAT // HALVES
+PARITIES = 2
+FREQS = FEAT // 2
+COS = 0
+SIN = 1
+ROPE_BASE = 10000.0
+RATIO = ROPE_BASE ** (-1.0 / FREQS)
+TURNS_PER_RADIAN = 1.0 / (2.0 * math.pi)
+ROUND_MAGIC = 1.5 * 2.0**23
+
+FLOPS = 2 * BATCH * SEQ * DIM * PROJECTIONS * FEAT
+
+
+def tile_ropemultiheadattention_pa_kernel(tc, x, Wq, bq, Wk, bk, out_0, out_1):
+    nc = tc.nc
+    weights = (Wq, Wk)
+    biases = (bq, bk)
+    outs = (out_0, out_1)
+
+    with ExitStack() as ctx:
+        keep = ctx.enter_context(tc.tile_pool(name="keep", bufs=1))
+        products = ctx.enter_context(tc.tile_pool(name="products", bufs=8))
+        results = ctx.enter_context(tc.tile_pool(name="results", bufs=3))
+        proj_psum = ctx.enter_context(tc.psum_pool(name="proj_psum", bufs=4))
+        flip_psum = ctx.enter_context(tc.psum_pool(name="flip_psum", bufs=4))
+
+        x_raw = keep.tile([P, BATCH, TOKEN_TILES, DIM], BF16)
+        w_raw = keep.tile([P, PROJECTIONS, PACK, FEAT], BF16)
+
+        def load_x(b):
+            nc.sync.dma_start(
+                out=x_raw[:, b], in_=x[b].rearrange("(c r) k -> c r k", r=TOKEN_TILES)
+            )
+
+        def load_w(w):
+            nc.sync.dma_start(
+                out=w_raw[:, w].rearrange("p (u v) i -> p u v i", u=2),
+                in_=weights[w].rearrange("(u p v) i -> p u v i", u=2, v=2),
+            )
+
+        load_x(0)
+        load_w(0)
+        load_x(1)
+        load_w(1)
+
+        bias = []
+        for w in range(PROJECTIONS):
+            bias_bf16 = keep.tile([P, HALVES, PARITIES], BF16, name="bias_bf16_%d" % w)
+            nc.scalar.dma_start(
+                out=bias_bf16[:],
+                in_=biases[w].rearrange("(h m e) -> m h e", h=HALVES, e=PARITIES),
+            )
+            bias.append(keep.tile([P, HALVES, PARITIES], F32, name="bias%d" % w))
+            nc.vector.tensor_copy(out=bias[w][:], in_=bias_bf16[:])
+
+        warm = keep.tile([P, 1], F32)
+        nc.vector.memset(warm[:], 0.0)
+        nc.scalar.activation(out=warm[:], in_=warm[:], func=ACT.Sin)
+
+        identity = keep.tile([P, P], F32)
+        make_identity(nc, identity[:])
+
+        token = keep.tile([P, TOKEN_TILES, P], F32)
+        nc.gpsimd.iota(
+            token[:],
+            pattern=[[1, TOKEN_TILES], [TOKEN_TILES, P]],
+            base=0,
+            channel_multiplier=0,
+            allow_small_or_imprecise_dtypes=True,
+        )
+
+        freq_row = keep.tile([P, FREQS], F32)
+        nc.vector.memset(freq_row[:, 0:1], 1.0)
+        done = 1
+        while done < FREQS:
+            nc.vector.tensor_scalar_mul(
+                out=freq_row[:, done : 2 * done], in0=freq_row[:, 0:done], scalar1=RATIO**done
+            )
+            done *= 2
+
+        freq_flip = flip_psum.tile([P, HALVES, P], F32, tag="flip")
+        for h in range(HALVES):
+            nc.tensor.transpose(freq_flip[:, h, :], freq_row[:, h * P : (h + 1) * P], identity[:])
+        freq = keep.tile([P, HALVES], F32)
+        nc.vector.tensor_scalar_mul(out=freq[:], in0=freq_flip[:, :, 0], scalar1=TURNS_PER_RADIAN)
+
+        tables = keep.tile([P, HALVES, 2, SEQ], F32)
+        turns = keep.tile([P, HALVES, 2, SEQ], F32)
+        whole = keep.tile([P, HALVES, 2, SEQ], F32)
+        excess = keep.tile([P, HALVES, 2, SEQ], F32)
+        for h in range(HALVES):
+            for kind in (COS, SIN):
+                nc.vector.tensor_scalar(
+                    out=turns[:, h, kind, :],
+                    in0=token[:].rearrange("p r c -> p (r c)"),
+                    scalar1=freq[:, h : h + 1],
+                    scalar2=0.25 if kind == COS else 0.0,
+                    op0=ALU.mult,
+                    op1=ALU.add,
+                )
+        for h in range(HALVES):
+            for kind in (COS, SIN):
+                nc.vector.tensor_scalar(
+                    out=whole[:, h, kind, :],
+                    in0=turns[:, h, kind, :],
+                    scalar1=ROUND_MAGIC,
+                    scalar2=ROUND_MAGIC,
+                    op0=ALU.add,
+                    op1=ALU.subtract,
+                )
+        for h in range(HALVES):
+            for kind in (COS, SIN):
+                nc.vector.tensor_sub(
+                    out=excess[:, h, kind, :], in0=whole[:, h, kind, :], in1=turns[:, h, kind, :]
+                )
+                negated = kind == SIN and h == 0
+                nc.scalar.activation(
+                    out=tables[:, h, kind, :],
+                    in_=excess[:, h, kind, :],
+                    func=ACT.Sin,
+                    scale=(2.0 if negated else -2.0) * math.pi,
+                )
+
+        x_grouped = keep.tile([P, BATCH, TOKEN_TILES, P, PACK], BF16, align_bytes=64)
+        x_codes = keep.tile([P, BATCH, SEQ], U32, align_bytes=64)
+        x_scales = keep.tile([P, BATCH, SEQ], U8, align_bytes=64)
+
+        def transpose_x(b):
+            x_words = x_raw[:, b].bitcast(F32)
+            for pair in range(TOKEN_PAIRS):
+                x_flip = flip_psum.tile([P, 2, 2, P], F32, tag="flip")
+                for r2 in range(2):
+                    for u in range(2):
+                        nc.tensor.transpose(
+                            x_flip[:, r2, u, :],
+                            x_words[:, 2 * pair + r2, u * P : (u + 1) * P],
+                            identity[:],
+                        )
+                nc.scalar.copy(
+                    out=x_grouped[:, b, 2 * pair : 2 * pair + 2, :, :].bitcast(F32),
+                    in_=x_flip[:].rearrange("p r u c -> p r c u"),
+                )
+
+        def quantise_x(b):
+            nc.vector.quantize_mx(
+                out=x_codes[:, b, :].bitcast(FP8X4),
+                scales=x_scales[:, b, :],
+                in_=x_grouped[:, b].rearrange("p r c t -> p (r c t)"),
+            )
+
+        w_codes = keep.tile([P, PROJECTIONS, FEAT], U32, align_bytes=64)
+        w_scales = keep.tile([P, PROJECTIONS, FEAT], U8, align_bytes=64)
+
+        def quantise_w(w):
+            w_grouped = keep.tile(
+                [P, HALVES, PARITIES, P, PACK], BF16, align_bytes=64, name="w_grouped%d" % w
+            )
+            by_parity = w_raw[:, w].rearrange("p t (h m e) -> p e h m t", h=HALVES, e=PARITIES)
+            nc.vector.tensor_copy(out=w_grouped[:, :, 0, :, :], in_=by_parity[:, 0])
+            nc.scalar.copy(out=w_grouped[:, :, 1, :, :], in_=by_parity[:, 1])
+            nc.vector.quantize_mx(
+                out=w_codes[:, w, :].bitcast(FP8X4),
+                scales=w_scales[:, w, :],
+                in_=w_grouped[:].rearrange("p h e m t -> p (h e m t)"),
+            )
+
+        def multiply(w, b, e):
+            proj = []
+            for h in range(HALVES):
+                tile_cols = slice((h * PARITIES + e) * P, (h * PARITIES + e + 1) * P)
+                proj.append(proj_psum.tile([P, SEQ], F32, tag="proj", name="proj"))
+                nc.tensor.matmul_mx(
+                    out=proj[h][:],
+                    lhsT=w_codes[:, w, tile_cols].bitcast(FP8X4),
+                    lhsT_scale=w_scales[:, w, tile_cols],
+                    rhs=x_codes[:, b, :].bitcast(FP8X4),
+                    rhs_scale=x_scales[:, b, :],
+                    start=True,
+                    stop=True,
+                )
+            return proj
+
+        def rotate(w, e, proj, back):
+            for h in range(HALVES):
+                by_cos = products.tile([P, SEQ], F32, tag="product")
+                nc.vector.scalar_tensor_tensor(
+                    out=by_cos[:],
+                    in0=proj[h][:],
+                    scalar=bias[w][:, h, e : e + 1],
+                    in1=tables[:, h, COS, :],
+                    op0=ALU.add,
+                    op1=ALU.mult,
+                )
+                by_sin = products.tile([P, SEQ], F32, tag="product")
+                nc.vector.scalar_tensor_tensor(
+                    out=by_sin[:],
+                    in0=proj[1 - h][:],
+                    scalar=bias[w][:, 1 - h, e : e + 1],
+                    in1=tables[:, h, SIN, :],
+                    op0=ALU.add,
+                    op1=ALU.mult,
+                )
+                for r in range(TOKEN_TILES):
+                    token_cols = slice(r * P, (r + 1) * P)
+                    for product, first in ((by_cos, True), (by_sin, False)):
+                        nc.tensor.matmul(
+                            out=back[h, r // 2][:, r % 2, e, :],
+                            lhsT=product[:, token_cols],
+                            rhs=identity[:],
+                            is_transpose=True,
+                            start=first,
+                            stop=not first,
+                        )
+
+        def store(w, b, back):
+            rotated = results.tile([P, TOKEN_TILES, FEAT], F32)
+            for h in range(HALVES):
+                for pair in range(TOKEN_PAIRS):
+                    nc.scalar.copy(
+                        out=rotated[
+                            :, 2 * pair : 2 * pair + 2, h * HALF : (h + 1) * HALF
+                        ].rearrange("c r (m e) -> c r m e", e=PARITIES),
+                        in_=back[h, pair][:].rearrange("c r e m -> c r m e"),
+                    )
+            for pair in range(TOKEN_PAIRS):
+                tiles = slice(2 * pair, 2 * pair + 2)
+                nc.sync.dma_start(
+                    out=outs[w][b].rearrange("(c r) i -> c r i", r=TOKEN_TILES)[:, tiles, :],
+                    in_=rotated[:, tiles, :],
+                )
+
+        transpose_x(0)
+        transpose_x(1)
+        quantise_x(0)
+        quantise_w(0)
+        quantise_x(1)
+        quantise_w(1)
+
+        steps = [
+            (w, b, e)
+            for w in range(PROJECTIONS)
+            for b in range(BATCH)
+            for e in range(PARITIES)
+        ]
+        proj = multiply(*steps[0])
+        back = {}
+        for step, (w, b, e) in enumerate(steps):
+            proj_next = multiply(*steps[step + 1]) if step + 1 < len(steps) else None
+            if e == 0:
+                for h in range(HALVES):
+                    for pair in range(TOKEN_PAIRS):
+                        back[h, pair] = flip_psum.tile(
+                            [P, 2, PARITIES, P], F32, tag="flip", name="back"
+                        )
+            rotate(w, e, proj, back)
+            if e == PARITIES - 1:
+                store(w, b, back)
+            proj = proj_next

@@ -27,6 +27,8 @@ PARITIES = 2
 FREQS = FEAT // 2
 COS = 0
 SIN = 1
+VECTOR_TILES = 1
+SPLIT = VECTOR_TILES * P
 ROPE_BASE = 10000.0
 RATIO = ROPE_BASE ** (-1.0 / FREQS)
 TURNS_PER_RADIAN = 1.0 / (2.0 * math.pi)
@@ -43,7 +45,8 @@ def tile_ropemultiheadattention_pa_kernel(tc, x, Wq, bq, Wk, bk, out_0, out_1):
 
     with ExitStack() as ctx:
         keep = ctx.enter_context(tc.tile_pool(name="keep", bufs=1))
-        products = ctx.enter_context(tc.tile_pool(name="products", bufs=8))
+        products = ctx.enter_context(tc.tile_pool(name="products", bufs=12))
+        shifted = ctx.enter_context(tc.tile_pool(name="shifted", bufs=3))
         results = ctx.enter_context(tc.tile_pool(name="results", bufs=3))
         proj_psum = ctx.enter_context(tc.psum_pool(name="proj_psum", bufs=4))
         flip_psum = ctx.enter_context(tc.psum_pool(name="flip_psum", bufs=4))
@@ -67,15 +70,13 @@ def tile_ropemultiheadattention_pa_kernel(tc, x, Wq, bq, Wk, bk, out_0, out_1):
         load_x(1)
         load_w(1)
 
-        bias = []
+        bias_bf16 = []
         for w in range(PROJECTIONS):
-            bias_bf16 = keep.tile([P, HALVES, PARITIES], BF16, name="bias_bf16_%d" % w)
+            bias_bf16.append(keep.tile([P, HALVES, PARITIES], BF16, name="bias_bf16_%d" % w))
             nc.scalar.dma_start(
-                out=bias_bf16[:],
+                out=bias_bf16[w][:],
                 in_=biases[w].rearrange("(h m e) -> m h e", h=HALVES, e=PARITIES),
             )
-            bias.append(keep.tile([P, HALVES, PARITIES], F32, name="bias%d" % w))
-            nc.vector.tensor_copy(out=bias[w][:], in_=bias_bf16[:])
 
         warm = keep.tile([P, 1], F32)
         nc.vector.memset(warm[:], 0.0)
@@ -92,6 +93,11 @@ def tile_ropemultiheadattention_pa_kernel(tc, x, Wq, bq, Wk, bk, out_0, out_1):
             channel_multiplier=0,
             allow_small_or_imprecise_dtypes=True,
         )
+
+        bias = []
+        for w in range(PROJECTIONS):
+            bias.append(keep.tile([P, HALVES, PARITIES], F32, name="bias%d" % w))
+            nc.gpsimd.tensor_copy(out=bias[w][:], in_=bias_bf16[w][:])
 
         freq_row = keep.tile([P, FREQS], F32)
         nc.vector.memset(freq_row[:, 0:1], 1.0)
@@ -188,7 +194,15 @@ def tile_ropemultiheadattention_pa_kernel(tc, x, Wq, bq, Wk, bk, out_0, out_1):
                 in_=w_grouped[:].rearrange("p h e m t -> p (h e m t)"),
             )
 
+        quantised = set()
+
         def multiply(w, b, e):
+            if ("x", b) not in quantised:
+                quantise_x(b)
+                quantised.add(("x", b))
+            if ("w", w) not in quantised:
+                quantise_w(w)
+                quantised.add(("w", w))
             proj = []
             for h in range(HALVES):
                 tile_cols = slice((h * PARITIES + e) * P, (h * PARITIES + e + 1) * P)
@@ -202,28 +216,37 @@ def tile_ropemultiheadattention_pa_kernel(tc, x, Wq, bq, Wk, bk, out_0, out_1):
                     start=True,
                     stop=True,
                 )
-            return proj
+            biased = shifted.tile([P, SEQ - SPLIT], F32)
+            nc.scalar.activation(
+                out=biased[:],
+                in_=proj[1][:, SPLIT:],
+                func=ACT.Identity,
+                bias=bias[w][:, 1, e : e + 1],
+                scale=1.0,
+            )
+            return proj, biased
 
-        def rotate(w, e, proj, back):
+        def rotate(w, e, proj, biased, back):
+            def times_table(source, table):
+                product = products.tile([P, SEQ], F32, tag="product")
+                vector_cols = slice(0, SEQ if source == 0 else SPLIT)
+                nc.vector.scalar_tensor_tensor(
+                    out=product[:, vector_cols],
+                    in0=proj[source][:, vector_cols],
+                    scalar=bias[w][:, source, e : e + 1],
+                    in1=table[:, vector_cols],
+                    op0=ALU.add,
+                    op1=ALU.mult,
+                )
+                if source == 1:
+                    nc.gpsimd.tensor_mul(
+                        out=product[:, SPLIT:], in0=biased[:], in1=table[:, SPLIT:]
+                    )
+                return product
+
             for h in range(HALVES):
-                by_cos = products.tile([P, SEQ], F32, tag="product")
-                nc.vector.scalar_tensor_tensor(
-                    out=by_cos[:],
-                    in0=proj[h][:],
-                    scalar=bias[w][:, h, e : e + 1],
-                    in1=tables[:, h, COS, :],
-                    op0=ALU.add,
-                    op1=ALU.mult,
-                )
-                by_sin = products.tile([P, SEQ], F32, tag="product")
-                nc.vector.scalar_tensor_tensor(
-                    out=by_sin[:],
-                    in0=proj[1 - h][:],
-                    scalar=bias[w][:, 1 - h, e : e + 1],
-                    in1=tables[:, h, SIN, :],
-                    op0=ALU.add,
-                    op1=ALU.mult,
-                )
+                by_cos = times_table(h, tables[:, h, COS, :])
+                by_sin = times_table(1 - h, tables[:, h, SIN, :])
                 for r in range(TOKEN_TILES):
                     token_cols = slice(r * P, (r + 1) * P)
                     for product, first in ((by_cos, True), (by_sin, False)):
@@ -255,10 +278,6 @@ def tile_ropemultiheadattention_pa_kernel(tc, x, Wq, bq, Wk, bk, out_0, out_1):
 
         transpose_x(0)
         transpose_x(1)
-        quantise_x(0)
-        quantise_w(0)
-        quantise_x(1)
-        quantise_w(1)
 
         steps = [
             (w, b, e)
@@ -266,17 +285,18 @@ def tile_ropemultiheadattention_pa_kernel(tc, x, Wq, bq, Wk, bk, out_0, out_1):
             for b in range(BATCH)
             for e in range(PARITIES)
         ]
-        proj = multiply(*steps[0])
+        ahead = multiply(*steps[0])
         back = {}
         for step, (w, b, e) in enumerate(steps):
-            proj_next = multiply(*steps[step + 1]) if step + 1 < len(steps) else None
+            proj, biased = ahead
+            if step + 1 < len(steps):
+                ahead = multiply(*steps[step + 1])
             if e == 0:
                 for h in range(HALVES):
                     for pair in range(TOKEN_PAIRS):
                         back[h, pair] = flip_psum.tile(
                             [P, 2, PARITIES, P], F32, tag="flip", name="back"
                         )
-            rotate(w, e, proj, back)
+            rotate(w, e, proj, biased, back)
             if e == PARITIES - 1:
                 store(w, b, back)
-            proj = proj_next

@@ -27,8 +27,6 @@ PARITIES = 2
 FREQS = FEAT // 2
 COS = 0
 SIN = 1
-VECTOR_TILES = 1
-SPLIT = VECTOR_TILES * P
 ROPE_BASE = 10000.0
 RATIO = ROPE_BASE ** (-1.0 / FREQS)
 TURNS_PER_RADIAN = 1.0 / (2.0 * math.pi)
@@ -45,11 +43,12 @@ def tile_ropemultiheadattention_pa_kernel(tc, x, Wq, bq, Wk, bk, out_0, out_1):
 
     with ExitStack() as ctx:
         keep = ctx.enter_context(tc.tile_pool(name="keep", bufs=1))
-        products = ctx.enter_context(tc.tile_pool(name="products", bufs=12))
-        shifted = ctx.enter_context(tc.tile_pool(name="shifted", bufs=3))
-        results = ctx.enter_context(tc.tile_pool(name="results", bufs=3))
+        products = ctx.enter_context(tc.tile_pool(name="products", bufs=8))
+        results = ctx.enter_context(tc.tile_pool(name="results", bufs=6))
         proj_psum = ctx.enter_context(tc.psum_pool(name="proj_psum", bufs=4))
         flip_psum = ctx.enter_context(tc.psum_pool(name="flip_psum", bufs=4))
+        ctx.enter_context(tc.manual_schedule())
+
 
         x_raw = keep.tile([P, BATCH, TOKEN_TILES, DIM], BF16)
         w_raw = keep.tile([P, PROJECTIONS, PACK, FEAT], BF16)
@@ -65,92 +64,8 @@ def tile_ropemultiheadattention_pa_kernel(tc, x, Wq, bq, Wk, bk, out_0, out_1):
                 in_=weights[w].rearrange("(u p v) i -> p u v i", u=2, v=2),
             )
 
-        load_x(0)
-        load_w(0)
-        load_x(1)
-        load_w(1)
-
-        bias_bf16 = []
-        for w in range(PROJECTIONS):
-            bias_bf16.append(keep.tile([P, HALVES, PARITIES], BF16, name="bias_bf16_%d" % w))
-            nc.scalar.dma_start(
-                out=bias_bf16[w][:],
-                in_=biases[w].rearrange("(h m e) -> m h e", h=HALVES, e=PARITIES),
-            )
-
-        warm = keep.tile([P, 1], F32)
-        nc.vector.memset(warm[:], 0.0)
-        nc.scalar.activation(out=warm[:], in_=warm[:], func=ACT.Sin)
-
         identity = keep.tile([P, P], F32)
-        make_identity(nc, identity[:])
-
-        token = keep.tile([P, TOKEN_TILES, P], F32)
-        nc.gpsimd.iota(
-            token[:],
-            pattern=[[1, TOKEN_TILES], [TOKEN_TILES, P]],
-            base=0,
-            channel_multiplier=0,
-            allow_small_or_imprecise_dtypes=True,
-        )
-
-        bias = []
-        for w in range(PROJECTIONS):
-            bias.append(keep.tile([P, HALVES, PARITIES], F32, name="bias%d" % w))
-            nc.gpsimd.tensor_copy(out=bias[w][:], in_=bias_bf16[w][:])
-
-        freq_row = keep.tile([P, FREQS], F32)
-        nc.vector.memset(freq_row[:, 0:1], 1.0)
-        done = 1
-        while done < FREQS:
-            nc.vector.tensor_scalar_mul(
-                out=freq_row[:, done : 2 * done], in0=freq_row[:, 0:done], scalar1=RATIO**done
-            )
-            done *= 2
-
-        freq_flip = flip_psum.tile([P, HALVES, P], F32, tag="flip")
-        for h in range(HALVES):
-            nc.tensor.transpose(freq_flip[:, h, :], freq_row[:, h * P : (h + 1) * P], identity[:])
-        freq = keep.tile([P, HALVES], F32)
-        nc.vector.tensor_scalar_mul(out=freq[:], in0=freq_flip[:, :, 0], scalar1=TURNS_PER_RADIAN)
-
-        tables = keep.tile([P, HALVES, 2, SEQ], F32)
-        turns = keep.tile([P, HALVES, 2, SEQ], F32)
-        whole = keep.tile([P, HALVES, 2, SEQ], F32)
-        excess = keep.tile([P, HALVES, 2, SEQ], F32)
-        for h in range(HALVES):
-            for kind in (COS, SIN):
-                nc.vector.tensor_scalar(
-                    out=turns[:, h, kind, :],
-                    in0=token[:].rearrange("p r c -> p (r c)"),
-                    scalar1=freq[:, h : h + 1],
-                    scalar2=0.25 if kind == COS else 0.0,
-                    op0=ALU.mult,
-                    op1=ALU.add,
-                )
-        for h in range(HALVES):
-            for kind in (COS, SIN):
-                nc.vector.tensor_scalar(
-                    out=whole[:, h, kind, :],
-                    in0=turns[:, h, kind, :],
-                    scalar1=ROUND_MAGIC,
-                    scalar2=ROUND_MAGIC,
-                    op0=ALU.add,
-                    op1=ALU.subtract,
-                )
-        for h in range(HALVES):
-            for kind in (COS, SIN):
-                nc.vector.tensor_sub(
-                    out=excess[:, h, kind, :], in0=whole[:, h, kind, :], in1=turns[:, h, kind, :]
-                )
-                negated = kind == SIN and h == 0
-                nc.scalar.activation(
-                    out=tables[:, h, kind, :],
-                    in_=excess[:, h, kind, :],
-                    func=ACT.Sin,
-                    scale=(2.0 if negated else -2.0) * math.pi,
-                )
-
+        x_flip = {}
         x_grouped = keep.tile([P, BATCH, TOKEN_TILES, P, PACK], BF16, align_bytes=64)
         x_codes = keep.tile([P, BATCH, SEQ], U32, align_bytes=64)
         x_scales = keep.tile([P, BATCH, SEQ], U8, align_bytes=64)
@@ -158,17 +73,20 @@ def tile_ropemultiheadattention_pa_kernel(tc, x, Wq, bq, Wk, bk, out_0, out_1):
         def transpose_x(b):
             x_words = x_raw[:, b].bitcast(F32)
             for pair in range(TOKEN_PAIRS):
-                x_flip = flip_psum.tile([P, 2, 2, P], F32, tag="flip")
+                x_flip[b, pair] = flip_psum.tile([P, 2, 2, P], F32, tag="flip", name="x_flip")
                 for r2 in range(2):
                     for u in range(2):
                         nc.tensor.transpose(
-                            x_flip[:, r2, u, :],
+                            x_flip[b, pair][:, r2, u, :],
                             x_words[:, 2 * pair + r2, u * P : (u + 1) * P],
                             identity[:],
                         )
+
+        def group_x(b):
+            for pair in range(TOKEN_PAIRS):
                 nc.scalar.copy(
                     out=x_grouped[:, b, 2 * pair : 2 * pair + 2, :, :].bitcast(F32),
-                    in_=x_flip[:].rearrange("p r u c -> p r c u"),
+                    in_=x_flip[b, pair][:].rearrange("p r u c -> p r c u"),
                 )
 
         def quantise_x(b):
@@ -178,31 +96,88 @@ def tile_ropemultiheadattention_pa_kernel(tc, x, Wq, bq, Wk, bk, out_0, out_1):
                 in_=x_grouped[:, b].rearrange("p r c t -> p (r c t)"),
             )
 
+        w_grouped = keep.tile([P, PROJECTIONS, HALVES, PARITIES, P, PACK], BF16, align_bytes=64)
         w_codes = keep.tile([P, PROJECTIONS, FEAT], U32, align_bytes=64)
         w_scales = keep.tile([P, PROJECTIONS, FEAT], U8, align_bytes=64)
 
-        def quantise_w(w):
-            w_grouped = keep.tile(
-                [P, HALVES, PARITIES, P, PACK], BF16, align_bytes=64, name="w_grouped%d" % w
-            )
+        def group_w(w):
             by_parity = w_raw[:, w].rearrange("p t (h m e) -> p e h m t", h=HALVES, e=PARITIES)
-            nc.vector.tensor_copy(out=w_grouped[:, :, 0, :, :], in_=by_parity[:, 0])
-            nc.scalar.copy(out=w_grouped[:, :, 1, :, :], in_=by_parity[:, 1])
+            for e in range(PARITIES):
+                nc.scalar.copy(out=w_grouped[:, w, :, e, :, :], in_=by_parity[:, e])
+
+        def quantise_w(w):
             nc.vector.quantize_mx(
                 out=w_codes[:, w, :].bitcast(FP8X4),
                 scales=w_scales[:, w, :],
-                in_=w_grouped[:].rearrange("p h e m t -> p (h e m t)"),
+                in_=w_grouped[:, w].rearrange("p h e m t -> p (h e m t)"),
             )
 
+        token = keep.tile([P, TOKEN_TILES, P], F32)
+        freq = keep.tile([P, HALVES], F32)
+        half_pi = keep.tile([P, 1], F32)
+        turns = keep.tile([P, HALVES, SEQ], F32)
+        whole = keep.tile([P, HALVES, SEQ], F32)
+        excess = keep.tile([P, HALVES, SEQ], F32)
+        size = keep.tile([P, HALVES, SEQ], F32)
+        tables = keep.tile([P, HALVES, 2, SEQ], F32)
+
+        def angle_in_turns(h):
+            nc.vector.tensor_scalar_mul(
+                out=turns[:, h, :],
+                in0=token[:].rearrange("p r c -> p (r c)"),
+                scalar1=freq[:, h : h + 1],
+            )
+
+        def round_turns(h):
+            nc.vector.tensor_scalar(
+                out=whole[:, h, :],
+                in0=turns[:, h, :],
+                scalar1=ROUND_MAGIC,
+                scalar2=ROUND_MAGIC,
+                op0=ALU.add,
+                op1=ALU.subtract,
+            )
+
+        def excess_of_turns(h):
+            nc.vector.tensor_sub(out=excess[:, h, :], in0=whole[:, h, :], in1=turns[:, h, :])
+
+        def size_of_excess(h):
+            nc.vector.scalar_tensor_tensor(
+                out=size[:, h, :],
+                in0=excess[:, h, :],
+                scalar=-1.0,
+                in1=excess[:, h, :],
+                op0=ALU.mult,
+                op1=ALU.max,
+            )
+
+        def sin_table(h):
+            nc.scalar.activation(
+                out=tables[:, h, SIN, :],
+                in_=excess[:, h, :],
+                func=ACT.Sin,
+                scale=(2.0 if h == 0 else -2.0) * math.pi,
+            )
+
+        def cos_table(h):
+            nc.scalar.activation(
+                out=tables[:, h, COS, :],
+                in_=size[:, h, :],
+                func=ACT.Sin,
+                scale=-2.0 * math.pi,
+                bias=half_pi[:],
+            )
+
+        bias = []
         quantised = set()
 
         def multiply(w, b, e):
-            if ("x", b) not in quantised:
-                quantise_x(b)
-                quantised.add(("x", b))
             if ("w", w) not in quantised:
                 quantise_w(w)
                 quantised.add(("w", w))
+            if ("x", b) not in quantised:
+                quantise_x(b)
+                quantised.add(("x", b))
             proj = []
             for h in range(HALVES):
                 tile_cols = slice((h * PARITIES + e) * P, (h * PARITIES + e + 1) * P)
@@ -216,69 +191,102 @@ def tile_ropemultiheadattention_pa_kernel(tc, x, Wq, bq, Wk, bk, out_0, out_1):
                     start=True,
                     stop=True,
                 )
-            biased = shifted.tile([P, SEQ - SPLIT], F32)
-            nc.scalar.activation(
-                out=biased[:],
-                in_=proj[1][:, SPLIT:],
-                func=ACT.Identity,
-                bias=bias[w][:, 1, e : e + 1],
-                scale=1.0,
-            )
-            return proj, biased
+            return proj
 
-        def rotate(w, e, proj, biased, back):
-            def times_table(source, table):
+        def rotate(w, e, h, proj, back):
+            summands = []
+            for source, kind in ((1 - h, SIN), (h, COS)):
                 product = products.tile([P, SEQ], F32, tag="product")
-                vector_cols = slice(0, SEQ if source == 0 else SPLIT)
                 nc.vector.scalar_tensor_tensor(
-                    out=product[:, vector_cols],
-                    in0=proj[source][:, vector_cols],
+                    out=product[:],
+                    in0=proj[source][:],
                     scalar=bias[w][:, source, e : e + 1],
-                    in1=table[:, vector_cols],
+                    in1=tables[:, h, kind, :],
                     op0=ALU.add,
                     op1=ALU.mult,
                 )
-                if source == 1:
-                    nc.gpsimd.tensor_mul(
-                        out=product[:, SPLIT:], in0=biased[:], in1=table[:, SPLIT:]
+                summands.append(product)
+            for r in range(TOKEN_TILES):
+                for product in summands:
+                    nc.tensor.matmul(
+                        out=back[h, r // 2][:, r % 2, e, :],
+                        lhsT=product[:, r * P : (r + 1) * P],
+                        rhs=identity[:],
+                        is_transpose=True,
+                        start=product is summands[0],
+                        stop=product is summands[-1],
                     )
-                return product
 
-            for h in range(HALVES):
-                by_cos = times_table(h, tables[:, h, COS, :])
-                by_sin = times_table(1 - h, tables[:, h, SIN, :])
-                for r in range(TOKEN_TILES):
-                    token_cols = slice(r * P, (r + 1) * P)
-                    for product, first in ((by_cos, True), (by_sin, False)):
-                        nc.tensor.matmul(
-                            out=back[h, r // 2][:, r % 2, e, :],
-                            lhsT=product[:, token_cols],
-                            rhs=identity[:],
-                            is_transpose=True,
-                            start=first,
-                            stop=not first,
-                        )
-
-        def store(w, b, back):
-            rotated = results.tile([P, TOKEN_TILES, FEAT], F32)
-            for h in range(HALVES):
-                for pair in range(TOKEN_PAIRS):
-                    nc.scalar.copy(
-                        out=rotated[
-                            :, 2 * pair : 2 * pair + 2, h * HALF : (h + 1) * HALF
-                        ].rearrange("c r (m e) -> c r m e", e=PARITIES),
-                        in_=back[h, pair][:].rearrange("c r e m -> c r m e"),
-                    )
+        def store(w, b, h, back):
             for pair in range(TOKEN_PAIRS):
-                tiles = slice(2 * pair, 2 * pair + 2)
+                rotated = results.tile([P, 2, HALF], F32)
+                nc.scalar.copy(
+                    out=rotated[:].rearrange("c r (m e) -> c r m e", e=PARITIES),
+                    in_=back[h, pair][:].rearrange("c r e m -> c r m e"),
+                )
                 nc.sync.dma_start(
-                    out=outs[w][b].rearrange("(c r) i -> c r i", r=TOKEN_TILES)[:, tiles, :],
-                    in_=rotated[:, tiles, :],
+                    out=outs[w][b].rearrange("(c r) i -> c r i", r=TOKEN_TILES)[
+                        :, 2 * pair : 2 * pair + 2, h * HALF : (h + 1) * HALF
+                    ],
+                    in_=rotated[:],
                 )
 
+
+        load_w(0)
+        load_x(0)
+        load_x(1)
+        load_w(1)
+
+        bias_bf16 = []
+        for w in range(PROJECTIONS):
+            bias_bf16.append(keep.tile([P, HALVES, PARITIES], BF16, name="bias_bf16_%d" % w))
+            nc.scalar.dma_start(
+                out=bias_bf16[w][:],
+                in_=biases[w].rearrange("(h m e) -> m h e", h=HALVES, e=PARITIES),
+            )
+
+        zero = keep.tile([P, 1], F32)
+        warm = keep.tile([P, 1], F32)
+        nc.vector.memset(zero[:], 0.0)
+        nc.scalar.activation(out=warm[:], in_=zero[:], func=ACT.Sin)
+
+        make_identity(nc, identity[:])
+        nc.gpsimd.iota(
+            token[:],
+            pattern=[[1, TOKEN_TILES], [TOKEN_TILES, P]],
+            base=0,
+            channel_multiplier=0,
+            allow_small_or_imprecise_dtypes=True,
+        )
+        for w in range(PROJECTIONS):
+            bias.append(keep.tile([P, HALVES, PARITIES], F32, name="bias%d" % w))
+            nc.gpsimd.tensor_copy(out=bias[w][:], in_=bias_bf16[w][:])
+
+        freq_row = keep.tile([P, FREQS], F32)
+        nc.vector.memset(freq_row[:, 0:1], 1.0)
+        done = 1
+        while done < FREQS:
+            nc.vector.tensor_scalar_mul(
+                out=freq_row[:, done : 2 * done], in0=freq_row[:, 0:done], scalar1=RATIO**done
+            )
+            done *= 2
+        nc.vector.tensor_scalar_add(out=half_pi[:], in0=zero[:], scalar1=math.pi / 2.0)
+
+        freq_flip = flip_psum.tile([P, HALVES, P], F32, tag="flip")
+        for h in range(HALVES):
+            nc.tensor.transpose(freq_flip[:, h, :], freq_row[:, h * P : (h + 1) * P], identity[:])
+        nc.vector.tensor_scalar_mul(out=freq[:], in0=freq_flip[:, :, 0], scalar1=TURNS_PER_RADIAN)
+
+        group_w(0)
         transpose_x(0)
         transpose_x(1)
-
+        group_x(0)
+        for table_step in (angle_in_turns, round_turns, excess_of_turns):
+            for h in range(HALVES):
+                table_step(h)
+        size_of_excess(0)
+        sin_table(0)
+        cos_table(0)
         steps = [
             (w, b, e)
             for w in range(PROJECTIONS)
@@ -286,17 +294,23 @@ def tile_ropemultiheadattention_pa_kernel(tc, x, Wq, bq, Wk, bk, out_0, out_1):
             for e in range(PARITIES)
         ]
         ahead = multiply(*steps[0])
+        size_of_excess(1)
+        sin_table(1)
+        cos_table(1)
+        group_x(1)
+        group_w(1)
+
         back = {}
         for step, (w, b, e) in enumerate(steps):
-            proj, biased = ahead
+            proj = ahead
             if step + 1 < len(steps):
                 ahead = multiply(*steps[step + 1])
-            if e == 0:
-                for h in range(HALVES):
+            for h in range(HALVES):
+                if e == 0:
                     for pair in range(TOKEN_PAIRS):
                         back[h, pair] = flip_psum.tile(
                             [P, 2, PARITIES, P], F32, tag="flip", name="back"
                         )
-            rotate(w, e, proj, biased, back)
-            if e == PARITIES - 1:
-                store(w, b, back)
+                rotate(w, e, h, proj, back)
+                if e == PARITIES - 1:
+                    store(w, b, h, back)

@@ -47,7 +47,6 @@ def tile_ropemultiheadattention_pa_kernel(tc, x, Wq, bq, Wk, bk, out_0, out_1):
         results = ctx.enter_context(tc.tile_pool(name="results", bufs=6))
         proj_psum = ctx.enter_context(tc.psum_pool(name="proj_psum", bufs=4))
         flip_psum = ctx.enter_context(tc.psum_pool(name="flip_psum", bufs=4))
-        ctx.enter_context(tc.manual_schedule())
 
 
         x_raw = keep.tile([P, BATCH, TOKEN_TILES, DIM], BF16)

@@ -27,6 +27,8 @@ PARITIES = 2
 FREQS = FEAT // 2
 COS = 0
 SIN = 1
+VECTOR_TILES = 2
+SPLIT = VECTOR_TILES * P
 ROPE_BASE = 10000.0
 RATIO = ROPE_BASE ** (-1.0 / FREQS)
 TURNS_PER_RADIAN = 1.0 / (2.0 * math.pi)
@@ -44,9 +46,11 @@ def tile_ropemultiheadattention_pa_kernel(tc, x, Wq, bq, Wk, bk, out_0, out_1):
     with ExitStack() as ctx:
         keep = ctx.enter_context(tc.tile_pool(name="keep", bufs=1))
         products = ctx.enter_context(tc.tile_pool(name="products", bufs=8))
+        shifted = ctx.enter_context(tc.tile_pool(name="shifted", bufs=3))
         results = ctx.enter_context(tc.tile_pool(name="results", bufs=6))
         proj_psum = ctx.enter_context(tc.psum_pool(name="proj_psum", bufs=4))
         flip_psum = ctx.enter_context(tc.psum_pool(name="flip_psum", bufs=4))
+        ctx.enter_context(tc.manual_schedule())
 
 
         x_raw = keep.tile([P, BATCH, TOKEN_TILES, DIM], BF16)
@@ -170,13 +174,16 @@ def tile_ropemultiheadattention_pa_kernel(tc, x, Wq, bq, Wk, bk, out_0, out_1):
         bias = []
         quantised = set()
 
-        def multiply(w, b, e):
+        def quantise_operands(w, b):
             if ("w", w) not in quantised:
                 quantise_w(w)
                 quantised.add(("w", w))
             if ("x", b) not in quantised:
                 quantise_x(b)
                 quantised.add(("x", b))
+
+        def multiply(w, b, e):
+            quantise_operands(w, b)
             proj = []
             for h in range(HALVES):
                 tile_cols = slice((h * PARITIES + e) * P, (h * PARITIES + e + 1) * P)
@@ -190,31 +197,47 @@ def tile_ropemultiheadattention_pa_kernel(tc, x, Wq, bq, Wk, bk, out_0, out_1):
                     start=True,
                     stop=True,
                 )
-            return proj
+            biased = shifted.tile([P, SEQ - SPLIT], F32)
+            nc.scalar.activation(
+                out=biased[:],
+                in_=proj[1][:, SPLIT:],
+                func=ACT.Identity,
+                bias=bias[w][:, 1, e : e + 1],
+                scale=1.0,
+            )
+            return proj, biased
 
-        def rotate(w, e, h, proj, back):
-            summands = []
-            for source, kind in ((1 - h, SIN), (h, COS)):
-                product = products.tile([P, SEQ], F32, tag="product")
-                nc.vector.scalar_tensor_tensor(
-                    out=product[:],
-                    in0=proj[source][:],
-                    scalar=bias[w][:, source, e : e + 1],
-                    in1=tables[:, h, kind, :],
-                    op0=ALU.add,
-                    op1=ALU.mult,
-                )
-                summands.append(product)
-            for r in range(TOKEN_TILES):
-                for product in summands:
-                    nc.tensor.matmul(
-                        out=back[h, r // 2][:, r % 2, e, :],
-                        lhsT=product[:, r * P : (r + 1) * P],
-                        rhs=identity[:],
-                        is_transpose=True,
-                        start=product is summands[0],
-                        stop=product is summands[-1],
+        def rotate(w, e, proj, biased, back):
+            product = {}
+            for source in range(HALVES):
+                for h, kind in ((1 - source, SIN), (source, COS)):
+                    product[h, kind] = products.tile([P, SEQ], F32, tag="product", name="product")
+                    vector_cols = slice(0, SEQ if source == 0 else SPLIT)
+                    nc.vector.scalar_tensor_tensor(
+                        out=product[h, kind][:, vector_cols],
+                        in0=proj[source][:, vector_cols],
+                        scalar=bias[w][:, source, e : e + 1],
+                        in1=tables[:, h, kind, vector_cols],
+                        op0=ALU.add,
+                        op1=ALU.mult,
                     )
+                    if source == 1:
+                        nc.gpsimd.tensor_mul(
+                            out=product[h, kind][:, SPLIT:],
+                            in0=biased[:],
+                            in1=tables[:, h, kind, SPLIT:],
+                        )
+            for h in range(HALVES):
+                for r in range(TOKEN_TILES):
+                    for kind in (SIN, COS):
+                        nc.tensor.matmul(
+                            out=back[h, r // 2][:, r % 2, e, :],
+                            lhsT=product[h, kind][:, r * P : (r + 1) * P],
+                            rhs=identity[:],
+                            is_transpose=True,
+                            start=kind == SIN,
+                            stop=kind == COS,
+                        )
 
         def store(w, b, h, back):
             for pair in range(TOKEN_PAIRS):
@@ -284,7 +307,7 @@ def tile_ropemultiheadattention_pa_kernel(tc, x, Wq, bq, Wk, bk, out_0, out_1):
             for h in range(HALVES):
                 table_step(h)
         size_of_excess(0)
-        sin_table(0)
+        sin_table(1)
         cos_table(0)
         steps = [
             (w, b, e)
@@ -292,24 +315,26 @@ def tile_ropemultiheadattention_pa_kernel(tc, x, Wq, bq, Wk, bk, out_0, out_1):
             for b in range(BATCH)
             for e in range(PARITIES)
         ]
-        ahead = multiply(*steps[0])
+        quantise_operands(*steps[0][:2])
         size_of_excess(1)
-        sin_table(1)
+        sin_table(0)
         cos_table(1)
+
+        multiplied = {0: multiply(*steps[0]), 1: multiply(*steps[1])}
         group_x(1)
         group_w(1)
-
         back = {}
         for step, (w, b, e) in enumerate(steps):
-            proj = ahead
-            if step + 1 < len(steps):
-                ahead = multiply(*steps[step + 1])
-            for h in range(HALVES):
-                if e == 0:
+            proj, biased = multiplied[step]
+            if e == 0:
+                for h in range(HALVES):
                     for pair in range(TOKEN_PAIRS):
                         back[h, pair] = flip_psum.tile(
                             [P, 2, PARITIES, P], F32, tag="flip", name="back"
                         )
-                rotate(w, e, h, proj, back)
-                if e == PARITIES - 1:
+            rotate(w, e, proj, biased, back)
+            if e == PARITIES - 1:
+                for h in range(HALVES):
                     store(w, b, h, back)
+            if step + 2 < len(steps):
+                multiplied[step + 2] = multiply(*steps[step + 2])

import math
from contextlib import ExitStack

import concourse.mybir as mybir
from concourse.masks import make_identity

F32 = mybir.dt.float32
BF16 = mybir.dt.bfloat16
U32 = mybir.dt.uint32
U8 = mybir.dt.uint8
FP8X4 = mybir.dt.float8_e4m3fn_x4
ALU = mybir.AluOpType
ACT = mybir.ActivationFunctionType

P = 128
PACK = 4
BATCH = 2
SEQ = 512
DIM = 512
FEAT = 512
PROJECTIONS = 2
TOKEN_TILES = SEQ // P
TOKEN_PAIRS = TOKEN_TILES // 2
HALVES = 2
HALF = FEAT // HALVES
PARITIES = 2
FREQS = FEAT // 2
COS = 0
SIN = 1
VECTOR_TILES = 2
SPLIT = VECTOR_TILES * P
ROPE_BASE = 10000.0
RATIO = ROPE_BASE ** (-1.0 / FREQS)
TURNS_PER_RADIAN = 1.0 / (2.0 * math.pi)
ROUND_MAGIC = 1.5 * 2.0**23

FLOPS = 2 * BATCH * SEQ * DIM * PROJECTIONS * FEAT


def tile_ropemultiheadattention_pa_kernel(tc, x, Wq, bq, Wk, bk, out_0, out_1):
    nc = tc.nc
    weights = (Wq, Wk)
    biases = (bq, bk)
    outs = (out_0, out_1)

    with ExitStack() as ctx:
        keep = ctx.enter_context(tc.tile_pool(name="keep", bufs=1))
        products = ctx.enter_context(tc.tile_pool(name="products", bufs=8))
        shifted = ctx.enter_context(tc.tile_pool(name="shifted", bufs=3))
        results = ctx.enter_context(tc.tile_pool(name="results", bufs=6))
        proj_psum = ctx.enter_context(tc.psum_pool(name="proj_psum", bufs=4))
        flip_psum = ctx.enter_context(tc.psum_pool(name="flip_psum", bufs=4))
        ctx.enter_context(tc.manual_schedule())


        x_raw = keep.tile([P, BATCH, TOKEN_TILES, DIM], BF16)
        w_raw = keep.tile([P, PROJECTIONS, PACK, FEAT], BF16)

        def load_x(b):
            nc.sync.dma_start(
                out=x_raw[:, b], in_=x[b].rearrange("(c r) k -> c r k", r=TOKEN_TILES)
            )

        def load_w(w):
            nc.sync.dma_start(
                out=w_raw[:, w].rearrange("p (u v) i -> p u v i", u=2),
                in_=weights[w].rearrange("(u p v) i -> p u v i", u=2, v=2),
            )

        identity = keep.tile([P, P], F32)
        x_flip = {}
        x_grouped = keep.tile([P, BATCH, TOKEN_TILES, P, PACK], BF16, align_bytes=64)
        x_codes = keep.tile([P, BATCH, SEQ], U32, align_bytes=64)
        x_scales = keep.tile([P, BATCH, SEQ], U8, align_bytes=64)

        def transpose_x(b):
            x_words = x_raw[:, b].bitcast(F32)
            for pair in range(TOKEN_PAIRS):
                x_flip[b, pair] = flip_psum.tile([P, 2, 2, P], F32, tag="flip", name="x_flip")
                for r2 in range(2):
                    for u in range(2):
                        nc.tensor.transpose(
                            x_flip[b, pair][:, r2, u, :],
                            x_words[:, 2 * pair + r2, u * P : (u + 1) * P],
                            identity[:],
                        )

        def group_x(b):
            for pair in range(TOKEN_PAIRS):
                nc.scalar.copy(
                    out=x_grouped[:, b, 2 * pair : 2 * pair + 2, :, :].bitcast(F32),
                    in_=x_flip[b, pair][:].rearrange("p r u c -> p r c u"),
                )

        def quantise_x(b):
            nc.vector.quantize_mx(
                out=x_codes[:, b, :].bitcast(FP8X4),
                scales=x_scales[:, b, :],
                in_=x_grouped[:, b].rearrange("p r c t -> p (r c t)"),
            )

        w_grouped = keep.tile([P, PROJECTIONS, HALVES, PARITIES, P, PACK], BF16, align_bytes=64)
        w_codes = keep.tile([P, PROJECTIONS, FEAT], U32, align_bytes=64)
        w_scales = keep.tile([P, PROJECTIONS, FEAT], U8, align_bytes=64)

        def group_w(w):
            by_parity = w_raw[:, w].rearrange("p t (h m e) -> p e h m t", h=HALVES, e=PARITIES)
            for e in range(PARITIES):
                nc.scalar.copy(out=w_grouped[:, w, :, e, :, :], in_=by_parity[:, e])

        def quantise_w(w):
            nc.vector.quantize_mx(
                out=w_codes[:, w, :].bitcast(FP8X4),
                scales=w_scales[:, w, :],
                in_=w_grouped[:, w].rearrange("p h e m t -> p (h e m t)"),
            )

        token = keep.tile([P, TOKEN_TILES, P], F32)
        freq = keep.tile([P, HALVES], F32)
        half_pi = keep.tile([P, 1], F32)
        turns = keep.tile([P, HALVES, SEQ], F32)
        whole = keep.tile([P, HALVES, SEQ], F32)
        excess = keep.tile([P, HALVES, SEQ], F32)
        size = keep.tile([P, HALVES, SEQ], F32)
        tables = keep.tile([P, HALVES, 2, SEQ], F32)

        def angle_in_turns(h):
            nc.vector.tensor_scalar_mul(
                out=turns[:, h, :],
                in0=token[:].rearrange("p r c -> p (r c)"),
                scalar1=freq[:, h : h + 1],
            )

        def round_turns(h):
            nc.vector.tensor_scalar(
                out=whole[:, h, :],
                in0=turns[:, h, :],
                scalar1=ROUND_MAGIC,
                scalar2=ROUND_MAGIC,
                op0=ALU.add,
                op1=ALU.subtract,
            )

        def excess_of_turns(h):
            nc.vector.tensor_sub(out=excess[:, h, :], in0=whole[:, h, :], in1=turns[:, h, :])

        def size_of_excess(h):
            nc.vector.scalar_tensor_tensor(
                out=size[:, h, :],
                in0=excess[:, h, :],
                scalar=-1.0,
                in1=excess[:, h, :],
                op0=ALU.mult,
                op1=ALU.max,
            )

        def sin_table(h):
            nc.scalar.activation(
                out=tables[:, h, SIN, :],
                in_=excess[:, h, :],
                func=ACT.Sin,
                scale=(2.0 if h == 0 else -2.0) * math.pi,
            )

        def cos_table(h):
            nc.scalar.activation(
                out=tables[:, h, COS, :],
                in_=size[:, h, :],
                func=ACT.Sin,
                scale=-2.0 * math.pi,
                bias=half_pi[:],
            )

        bias = []
        quantised = set()

        def quantise_operands(w, b):
            if ("w", w) not in quantised:
                quantise_w(w)
                quantised.add(("w", w))
            if ("x", b) not in quantised:
                quantise_x(b)
                quantised.add(("x", b))

        def multiply(w, b, e):
            quantise_operands(w, b)
            proj = []
            for h in range(HALVES):
                tile_cols = slice((h * PARITIES + e) * P, (h * PARITIES + e + 1) * P)
                proj.append(proj_psum.tile([P, SEQ], F32, tag="proj", name="proj"))
                nc.tensor.matmul_mx(
                    out=proj[h][:],
                    lhsT=w_codes[:, w, tile_cols].bitcast(FP8X4),
                    lhsT_scale=w_scales[:, w, tile_cols],
                    rhs=x_codes[:, b, :].bitcast(FP8X4),
                    rhs_scale=x_scales[:, b, :],
                    start=True,
                    stop=True,
                )
            biased = shifted.tile([P, SEQ - SPLIT], F32)
            nc.scalar.activation(
                out=biased[:],
                in_=proj[1][:, SPLIT:],
                func=ACT.Identity,
                bias=bias[w][:, 1, e : e + 1],
                scale=1.0,
            )
            return proj, biased

        def rotate(w, e, proj, biased, back):
            product = {}
            for source in range(HALVES):
                for h, kind in ((1 - source, SIN), (source, COS)):
                    product[h, kind] = products.tile([P, SEQ], F32, tag="product", name="product")
                    vector_cols = slice(0, SEQ if source == 0 else SPLIT)
                    nc.vector.scalar_tensor_tensor(
                        out=product[h, kind][:, vector_cols],
                        in0=proj[source][:, vector_cols],
                        scalar=bias[w][:, source, e : e + 1],
                        in1=tables[:, h, kind, vector_cols],
                        op0=ALU.add,
                        op1=ALU.mult,
                    )
                    if source == 1:
                        nc.gpsimd.tensor_mul(
                            out=product[h, kind][:, SPLIT:],
                            in0=biased[:],
                            in1=tables[:, h, kind, SPLIT:],
                        )
            for h in range(HALVES):
                for r in range(TOKEN_TILES):
                    for kind in (SIN, COS):
                        nc.tensor.matmul(
                            out=back[h, r // 2][:, r % 2, e, :],
                            lhsT=product[h, kind][:, r * P : (r + 1) * P],
                            rhs=identity[:],
                            is_transpose=True,
                            start=kind == SIN,
                            stop=kind == COS,
                        )

        def store(w, b, h, back):
            for pair in range(TOKEN_PAIRS):
                rotated = results.tile([P, 2, HALF], F32)
                nc.scalar.copy(
                    out=rotated[:].rearrange("c r (m e) -> c r m e", e=PARITIES),
                    in_=back[h, pair][:].rearrange("c r e m -> c r m e"),
                )
                nc.sync.dma_start(
                    out=outs[w][b].rearrange("(c r) i -> c r i", r=TOKEN_TILES)[
                        :, 2 * pair : 2 * pair + 2, h * HALF : (h + 1) * HALF
                    ],
                    in_=rotated[:],
                )


        load_w(0)
        load_x(0)
        load_x(1)
        load_w(1)

        bias_bf16 = []
        for w in range(PROJECTIONS):
            bias_bf16.append(keep.tile([P, HALVES, PARITIES], BF16, name="bias_bf16_%d" % w))
            nc.scalar.dma_start(
                out=bias_bf16[w][:],
                in_=biases[w].rearrange("(h m e) -> m h e", h=HALVES, e=PARITIES),
            )

        zero = keep.tile([P, 1], F32)
        warm = keep.tile([P, 1], F32)
        nc.vector.memset(zero[:], 0.0)
        nc.scalar.activation(out=warm[:], in_=zero[:], func=ACT.Sin)

        make_identity(nc, identity[:])
        nc.gpsimd.iota(
            token[:],
            pattern=[[1, TOKEN_TILES], [TOKEN_TILES, P]],
            base=0,
            channel_multiplier=0,
            allow_small_or_imprecise_dtypes=True,
        )
        for w in range(PROJECTIONS):
            bias.append(keep.tile([P, HALVES, PARITIES], F32, name="bias%d" % w))
            nc.gpsimd.tensor_copy(out=bias[w][:], in_=bias_bf16[w][:])

        freq_row = keep.tile([P, FREQS], F32)
        nc.vector.memset(freq_row[:, 0:1], 1.0)
        done = 1
        while done < FREQS:
            nc.vector.tensor_scalar_mul(
                out=freq_row[:, done : 2 * done], in0=freq_row[:, 0:done], scalar1=RATIO**done
            )
            done *= 2
        nc.vector.tensor_scalar_add(out=half_pi[:], in0=zero[:], scalar1=math.pi / 2.0)

        freq_flip = flip_psum.tile([P, HALVES, P], F32, tag="flip")
        for h in range(HALVES):
            nc.tensor.transpose(freq_flip[:, h, :], freq_row[:, h * P : (h + 1) * P], identity[:])
        nc.vector.tensor_scalar_mul(out=freq[:], in0=freq_flip[:, :, 0], scalar1=TURNS_PER_RADIAN)

        group_w(0)
        transpose_x(0)
        transpose_x(1)
        group_x(0)
        for table_step in (angle_in_turns, round_turns, excess_of_turns):
            for h in range(HALVES):
                table_step(h)
        size_of_excess(0)
        sin_table(1)
        cos_table(0)
        steps = [
            (w, b, e)
            for w in range(PROJECTIONS)
            for b in range(BATCH)
            for e in range(PARITIES)
        ]
        quantise_operands(*steps[0][:2])
        size_of_excess(1)
        sin_table(0)
        cos_table(1)

        multiplied = {0: multiply(*steps[0]), 1: multiply(*steps[1])}
        group_x(1)
        group_w(1)
        back = {}
        for step, (w, b, e) in enumerate(steps):
            proj, biased = multiplied[step]
            if e == 0:
                for h in range(HALVES):
                    for pair in range(TOKEN_PAIRS):
                        back[h, pair] = flip_psum.tile(
                            [P, 2, PARITIES, P], F32, tag="flip", name="back"
                        )
            rotate(w, e, proj, biased, back)
            if e == PARITIES - 1:
                for h in range(HALVES):
                    store(w, b, h, back)
            if step + 2 < len(steps):
                multiplied[step + 2] = multiply(*steps[step + 2])
